import numpy as np
import ml_dtypes


def mxq(x, axis, fmt="e4m3"):
    dtype, down = {"e4m3": (ml_dtypes.float8_e4m3fn, 7), "e5m2": (ml_dtypes.float8_e5m2, 14)}[fmt]
    v = np.moveaxis(np.asarray(x, np.float32).astype(ml_dtypes.bfloat16).astype(np.float64), axis, -1)
    blocks = v.reshape(v.shape[:-1] + (-1, 32))
    amax = np.abs(blocks).max(-1, keepdims=True)
    byte = np.maximum(np.where(amax > 0, np.frexp(amax)[1] - 1 + 127, 0) - down, 1)
    scale = np.exp2(byte - 127.0)
    codes = (blocks / scale).astype(np.float32).astype(dtype).astype(np.float64)
    return np.moveaxis((codes * scale).reshape(v.shape), -1, axis)


WIDE = False


def mx_kscale(k):
    if not WIDE:
        return np.ones(k)
    levels = np.array([10, -10, 5, -5, 0])
    if k % 512:
        return np.exp2(np.random.permutation(np.resize(levels, k // 32))).repeat(32)
    a = np.empty((k // 512, 16))
    for p in range(k // 512):
        a[p, :8] = np.random.permutation(np.resize(levels, 8))
        for g in range(8):
            far = levels[np.abs(levels - a[p, g]) >= 10]
            a[p, g + 8] = far[np.random.randint(len(far))]
    return np.exp2(a.ravel()).repeat(32)


BF16 = ml_dtypes.bfloat16


def bf(x):
    return np.asarray(x, np.float32).astype(BF16)


def f64(x):
    return np.asarray(x).astype(np.float64)


E2M1 = np.array([0.0, 0.5, 1.0, 1.5, 2.0, 3.0, 4.0, 6.0, -0.0, -0.5, -1.0, -1.5, -2.0, -3.0, -4.0, -6.0])


def pack_weight(w, fmt):
    k, n = w.shape
    w = f64(bf(w)).reshape(k // 32, 32, n)
    amax = np.abs(w).max(1)
    if fmt == "e4m3":
        byte = np.frexp(amax)[1] - 1 + 127 - 7
    else:
        mant, ex = np.frexp(amax / 6.0)
        byte = np.where(mant > 0.5, ex, ex - 1) + 127
    byte = np.clip(np.where(amax > 0, byte, 1), 1, 254)
    scaled = (w * np.exp2(127.0 - byte)[:, None, :]).reshape(k, n).astype(np.float32)
    by_word = np.ascontiguousarray(scaled.reshape(k // 512, 128, 4, n).transpose(0, 1, 3, 2))
    if fmt == "e4m3":
        words = by_word.astype(ml_dtypes.float8_e4m3fn).view(np.uint8)
    else:
        c = by_word.astype(ml_dtypes.float4_e2m1fn).view(np.uint8) & 0xF
        words = c[..., 0::2] | (c[..., 1::2] << 4)
    return np.ascontiguousarray(words), np.ascontiguousarray(byte.astype(np.uint8).reshape(k // 512, 16, n))


def unpack_weight(words, scales, fmt):
    g, p, n, _ = words.shape
    if fmt == "e4m3":
        vals = np.ascontiguousarray(words).view(ml_dtypes.float8_e4m3fn).astype(np.float64)
    else:
        nib = np.empty((g, p, n, 4), np.uint8)
        nib[..., 0::2] = words & 0xF
        nib[..., 1::2] = words >> 4
        vals = E2M1[nib]
    vals = vals * np.repeat(np.exp2(scales.astype(np.float64) - 127.0), 8, axis=1)[..., None]
    return vals.transpose(0, 1, 3, 2).reshape(g * 512, n)
def pack4(w):
    words, scales = pack_weight(w, "e2m1")
    return words.reshape(words.shape[0], 128, -1), scales


def unpack4(words, scales):
    return unpack_weight(words.reshape(words.shape[0], 128, -1, 2), scales, "e2m1")


B, S, D, H = 16, 256, 512, 2


def draw0():
    s = mx_kscale(D)
    t = np.tile(mx_kscale(D), H)
    x = bf(np.random.standard_normal((B, S, D)) * s)
    Wq_words, Wq_scales = pack4(np.random.standard_normal((D, H * D)) * 1.4 / np.sqrt(D) / s[:, None] * t)
    Wk_words, Wk_scales = pack4(np.random.standard_normal((D, H * D)) * 1.4 / np.sqrt(D) / s[:, None] / t)
    return {"x": x,
            "Wq_words": Wq_words, "Wq_scales": Wq_scales,
            "Wk_words": Wk_words, "Wk_scales": Wk_scales}


def core(x, Wq_words, Wq_scales, Wk_words, Wk_scales):
    xq = mxq(f64(x), 2, "e4m3")
    Q = np.reshape(xq @ unpack4(Wq_words, Wq_scales), (B, H, S, D))
    K = np.reshape(xq @ unpack4(Wk_words, Wk_scales), (B, H, S, D))
    scores = mxq(Q, 3, "e4m3") @ mxq(K, 3, "e4m3").transpose(0, 1, 3, 2)
    z = scores / np.sqrt(D)
    e = np.exp(z - z.max(-1, keepdims=True))
    return e / e.sum(-1, keepdims=True)


def e4m3fn_bytes(y):
    return np.clip(np.asarray(y, np.float64), -448.0, 448.0).astype(np.float32).astype(ml_dtypes.float8_e4m3fn).view(np.uint8)


def e4m3fn_values(b):
    return np.asarray(b, np.uint8).view(ml_dtypes.float8_e4m3fn).astype(np.float64)


def setup_inputs():
    d = draw0()
    x0 = np.asarray(d['x']).astype(np.float64)
    s = (np.max(np.abs(x0), axis=(0, 1), keepdims=True) / 448.0).astype(np.float32)
    out = {}
    for k, v in d.items():
        if k == 'x':
            out['x_bytes'] = e4m3fn_bytes(x0 / s.astype(np.float64))
            out['x_scale'] = s
        else:
            out[k] = v
    return out


def reference(x_bytes, x_scale, Wq_words, Wq_scales, Wk_words, Wk_scales):
    return core(e4m3fn_values(x_bytes) * x_scale.astype(np.float64), Wq_words, Wq_scales, Wk_words, Wk_scales)

@@ -1,0 +1,297 @@
+import math
+from contextlib import ExitStack
+
+import concourse.mybir as mybir
+from concourse.masks import make_identity
+
+B, S, D, H = 16, 256, 512, 2
+P = 128
+PACK = 4
+UNITS = B * H
+N_OUT = H * D
+
+F32 = mybir.dt.float32
+BF16 = mybir.dt.bfloat16
+I32 = mybir.dt.int32
+U32 = mybir.dt.uint32
+U8 = mybir.dt.uint8
+FP8 = mybir.dt.float8_e4m3fn
+FP8X4 = mybir.dt.float8_e4m3fn_x4
+FP4X4 = mybir.dt.float4_e2m1fn_x4
+ACT = mybir.ActivationFunctionType
+ALU = mybir.AluOpType
+AX = mybir.AxisListType
+
+FLOPS = 2 * B * S * D * N_OUT * 2 + 2 * B * H * S * S * D
+
+X_CHUNKS = (2, 2, 4, 8, 8, 8)
+
+
+def tile_bertselfattention_pa_t_w4_kernel(
+    tc, x_bytes, x_scale, wq_words, wq_scales, wk_words, wk_scales, out
+):
+    nc = tc.nc
+    inv = 1.0 / math.sqrt(D)
+
+    with ExitStack() as ctx:
+        keep = ctx.enter_context(tc.tile_pool(name="keep", bufs=1))
+        xin = ctx.enter_context(tc.tile_pool(name="xin", bufs=1))
+        work = ctx.enter_context(tc.tile_pool(name="work", bufs=3))
+        small = ctx.enter_context(tc.tile_pool(name="small", bufs=4))
+        ps_tr = ctx.enter_context(tc.psum_pool(name="ps_tr", bufs=1))
+        ps_pj = ctx.enter_context(tc.psum_pool(name="ps_pj", bufs=5))
+        ps_sc = ctx.enter_context(tc.psum_pool(name="ps_sc", bufs=2))
+        ctx.enter_context(tc.manual_schedule())
+
+        x_view = x_bytes.rearrange("b (h p) k -> p (b h) k", p=P)
+        x_of = {}
+
+        def load_x(i):
+            u0 = sum(X_CHUNKS[:i])
+            n = X_CHUNKS[i]
+            xbytes = xin.tile([P, n * D], U8, name="xbytes%d" % i, align_bytes=64)
+            nc.sync.dma_start(
+                out=xbytes[:].rearrange("p (u k) -> p u k", u=n), in_=x_view[:, u0 : u0 + n, :]
+            )
+            for j in range(n):
+                x_of[u0 + j] = (xbytes, j)
+
+        raw_s = keep.tile([P, 2 * N_OUT], U8, name="raw_s", align_bytes=64)
+        nc.vector.memset(raw_s[:].bitcast(I32), 0)
+        xs_col = keep.tile([P, PACK], F32, name="xs_col")
+        nc.scalar.dma_start(
+            out=xs_col[:], in_=x_scale.rearrange("a o (p t) -> p (a o t)", t=PACK)
+        )
+        ident = keep.tile([P, P], F32, name="ident", align_bytes=64)
+        make_identity(nc, ident[:])
+        warm = keep.tile([P, 1], F32, name="warm")
+        nc.vector.memset(warm[:], 0.0)
+        warm_out = keep.tile([P, 1], F32, name="warm_out")
+        nc.scalar.activation(out=warm_out[:], in_=warm[:], func=ACT.Exp)
+
+        load_x(0)
+        raw_w = []
+        for w, (words, scales) in enumerate(((wq_words, wq_scales), (wk_words, wk_scales))):
+            rw = keep.tile([P, 2 * N_OUT], U8, name="raw_w%d" % w, align_bytes=64)
+            nc.sync.dma_start(out=rw[:].bitcast(I32), in_=words[0].bitcast(I32))
+            raw_w.append(rw)
+            for q in range(4):
+                nc.sync.dma_start(
+                    out=raw_s[32 * q : 32 * q + 4, w * N_OUT : (w + 1) * N_OUT].bitcast(I32),
+                    in_=scales[0, 4 * q : 4 * q + 4, :].bitcast(I32),
+                )
+        for i in range(1, len(X_CHUNKS)):
+            load_x(i)
+
+        w_codes = []
+        w_scales = []
+
+        def permute(w):
+            wc = keep.tile([P, 2 * N_OUT], U8, name="wc%d" % w, align_bytes=64)
+            ws = keep.tile([P, N_OUT], U8, name="ws%d" % w, align_bytes=64)
+            dst_c = wc[:].bitcast(I32).rearrange("p (h t q c) -> p h q t c", h=2, t=4, q=16)
+            src_c = raw_w[w][:].bitcast(I32).rearrange("p (h q t c) -> p h q t c", h=2, t=4, q=16)
+            dst_s = ws[:].bitcast(I32).rearrange("p (h t q c) -> p h q t c", h=2, t=4, q=16)
+            src_s = (
+                raw_s[:, w * N_OUT : (w + 1) * N_OUT]
+                .bitcast(I32)
+                .rearrange("p (h q t c) -> p h q t c", h=2, t=4, q=16)
+            )
+            for h in range(2):
+                nc.vector.tensor_copy(out=dst_c[:, h], in_=src_c[:, h])
+                nc.vector.tensor_copy(out=dst_s[:, h], in_=src_s[:, h])
+            w_codes.append(wc)
+            w_scales.append(ws)
+
+        st = {}
+
+        def cast(u):
+            xbytes, j = x_of[u]
+            xb = work.tile([P, 2 * D], BF16, name="xb", align_bytes=64)
+            nc.vector.tensor_copy(out=xb[:], in_=xbytes[:, j * D : (j + 2) * D].bitcast(FP8))
+            st["xb", u] = xb
+
+        def trans(u):
+            tr = ps_tr.tile([P, 2, 2, P], F32, name="tr")
+            words = st["xb", u][:].bitcast(F32)
+            for v in range(2):
+                for e in range(2):
+                    nc.tensor.transpose(
+                        tr[:, e, v, :], words[:, v * (D // 2) + e : (v + 1) * (D // 2) : 2], ident[:]
+                    )
+            st["tr", u] = tr
+
+        def mult(u):
+            xg = work.tile([P, 2 * P, PACK], BF16, name="xg", align_bytes=64)
+            nc.vector.tensor_tensor(
+                out=xg[:].rearrange("p n (e c) -> p n e c", e=2),
+                in0=st["tr", u][:].rearrange("p e v n -> p e (v n)").bitcast(BF16).rearrange("p e (n c) -> p n e c", c=2),
+                in1=xs_col[:].rearrange("p (e c) -> p e c", e=2).unsqueeze(1).to_broadcast([P, 2 * P, 2, 2]),
+                op=ALU.mult,
+            )
+            st["xg", u] = xg
+
+        def quant_x(u):
+            xc = work.tile([P, 2 * P], U32, name="xc", align_bytes=64)
+            xs = work.tile([P, 2 * P], U8, name="xs", align_bytes=64)
+            nc.vector.quantize_mx(
+                out=xc[:].bitcast(FP8X4),
+                scales=xs[:],
+                in_=st["xg", u][:].rearrange("p n t -> p (n t)"),
+            )
+            for v in range(2):
+                st["xq", u + v] = (xc[:, v * P : (v + 1) * P], xs[:, v * P : (v + 1) * P])
+
+        def proj(u, c):
+            w, h = divmod(c, 2)
+            xc, xs = st["xq", u]
+            pj = ps_pj.tile([P, PACK, P], F32, name="pj")
+            for t in range(PACK):
+                col = (h * PACK + t) * P
+                nc.tensor.matmul_mx(
+                    out=pj[:, t, :],
+                    lhsT=w_codes[w][:, 2 * col : 2 * (col + P)].bitcast(FP4X4),
+                    lhsT_scale=w_scales[w][:, col : col + P],
+                    rhs=xc.bitcast(FP8X4),
+                    rhs_scale=xs,
+                    start=True,
+                    stop=True,
+                )
+            st["pj", u, c] = pj
+
+        def copy(u, c):
+            if c == 0:
+                st["qk", u] = work.tile([P, 4, P, PACK], BF16, name="qk", align_bytes=64)
+            dst = st["qk", u][:, c]
+            src = st["pj", u, c][:].rearrange("p t n -> p n t")
+            if c == 2 and u % 2 == 1:
+                nc.vector.tensor_copy(out=dst, in_=src)
+            else:
+                nc.scalar.copy(out=dst, in_=src)
+
+        def quant_qk(u):
+            qc = work.tile([P, 4 * P], U32, name="qc", align_bytes=64)
+            qs = work.tile([P, 4 * P], U8, name="qs", align_bytes=64)
+            nc.vector.quantize_mx(
+                out=qc[:].bitcast(FP8X4),
+                scales=qs[:],
+                in_=st["qk", u][:].rearrange("p c n t -> p (c n t)"),
+            )
+            st["qq", u] = (qc, qs)
+
+        def scores(u):
+            qc, qs = st["qq", u]
+            sc = ps_sc.tile([P, 2, S], F32, name="sc")
+            for h in range(2):
+                nc.tensor.matmul_mx(
+                    out=sc[:, h, :],
+                    lhsT=qc[:, h * P : (h + 1) * P].bitcast(FP8X4),
+                    lhsT_scale=qs[:, h * P : (h + 1) * P],
+                    rhs=qc[:, 2 * P : 4 * P].bitcast(FP8X4),
+                    rhs_scale=qs[:, 2 * P : 4 * P],
+                    start=True,
+                    stop=True,
+                )
+            st["sc", u] = sc
+
+        def rowmax(u):
+            mx = small.tile([P, 2], F32, name="mx")
+            nc.vector.tensor_reduce(out=mx[:], in_=st["sc", u][:], axis=AX.X, op=ALU.max)
+            st["mx", u] = mx
+
+        def negb(u):
+            nb = small.tile([P, 2], F32, name="nb")
+            nc.gpsimd.tensor_scalar(
+                out=nb[:], in0=st["mx", u][:], scalar1=-inv, scalar2=None, op0=ALU.mult
+            )
+            st["nb", u] = nb
+
+        def expo(u, h):
+            v = u % 2
+            if h == 0 and v == 0:
+                st["ex", u // 2] = work.tile([P, 2, 2, S], F32, name="ex", align_bytes=64)
+                st["sm", u // 2] = small.tile([P, 2, 2], F32, name="sm")
+            nc.scalar.activation(
+                out=st["ex", u // 2][:, v, h, :].rearrange("p (n g) -> p n g", g=2),
+                in_=st["sc", u][:, h, :].rearrange("p (g n) -> p n g", g=2),
+                func=ACT.Exp,
+                bias=st["nb", u][:, h : h + 1],
+                scale=inv,
+                accum_out=st["sm", u // 2][:, v, h : h + 1],
+            )
+
+        def recip(m, v0, v1):
+            if v0 == 0:
+                st["ri", m] = small.tile([P, 2, 2], F32, name="ri")
+            nc.vector.reciprocal(out=st["ri", m][:, v0:v1, :], in_=st["sm", m][:, v0:v1, :])
+
+        def norm(m, v0, v1):
+            if v0 == 0:
+                st["o", m] = work.tile([P, 2, 2, S], F32, name="o", align_bytes=64)
+            o = st["o", m]
+            for v in range(v0, v1):
+                for h in range(2):
+                    nc.gpsimd.tensor_scalar(
+                        out=o[:, v, h, :],
+                        in0=st["ex", m][:, v, h, :],
+                        scalar1=st["ri", m][:, v, h : h + 1],
+                        scalar2=0.0,
+                        op0=ALU.mult,
+                        op1=ALU.add,
+                    )
+            nc.sync.dma_start(
+                out=out[m, v0:v1].rearrange("v (p f) j -> p v (f j)", f=2),
+                in_=o[:, v0:v1].rearrange("p v f j -> p v (f j)"),
+            )
+
+        def live(u):
+            return 0 <= u < UNITS
+
+        for s in range(-3, UNITS + 3):
+            odd = s % 2 == 1
+            if live(s - 1):
+                quant_qk(s - 1)
+            if live(s + 1):
+                proj(s + 1, 0)
+            if live(s - 1):
+                scores(s - 1)
+            if odd and live(s + 3):
+                cast(s + 3)
+            if not odd and live(s + 2):
+                mult(s + 2)
+            if live(s):
+                copy(s, 0)
+            if live(s - 1):
+                rowmax(s - 1)
+                negb(s - 1)
+            if live(s - 2):
+                expo(s - 2, 0)
+            if live(s + 1):
+                proj(s + 1, 1)
+            if live(s):
+                copy(s, 1)
+            if live(s - 2):
+                expo(s - 2, 1)
+            if live(s):
+                copy(s, 2)
+            if live(s + 1):
+                proj(s + 1, 2)
+            if odd and live(s + 3):
+                trans(s + 3)
+            if not odd and live(s + 2):
+                quant_x(s + 2)
+            if s == -3:
+                permute(0)
+            if s == -2:
+                permute(1)
+            if live(s):
+                copy(s, 3)
+            if live(s + 1):
+                proj(s + 1, 3)
+            if live(s - 2):
+                if s - 2 >= UNITS - 2:
+                    recip((s - 2) // 2, s % 2, s % 2 + 1)
+                    norm((s - 2) // 2, s % 2, s % 2 + 1)
+                elif odd:
+                    recip((s - 2) // 2, 0, 2)
+                    norm((s - 2) // 2, 0, 2)

@@ -164,7 +164,7 @@ def tile_bertselfattention_pa_t_w4_kernel(
                 st["qk", u] = work.tile([P, 4, P, PACK], BF16, name="qk", align_bytes=64)
             dst = st["qk", u][:, c]
             src = st["pj", u, c][:].rearrange("p t n -> p n t")
-            if c == 2 and u % 2 == 1:
+            if False:
                 nc.vector.tensor_copy(out=dst, in_=src)
             else:
                 nc.scalar.copy(out=dst, in_=src)
@@ -201,7 +201,7 @@ def tile_bertselfattention_pa_t_w4_kernel(
 
         def negb(u):
             nb = small.tile([P, 2], F32, name="nb")
-            nc.gpsimd.tensor_scalar(
+            nc.vector.tensor_scalar(
                 out=nb[:], in0=st["mx", u][:], scalar1=-inv, scalar2=None, op0=ALU.mult
             )
             st["nb", u] = nb
@@ -231,13 +231,12 @@ def tile_bertselfattention_pa_t_w4_kernel(
             o = st["o", m]
             for v in range(v0, v1):
                 for h in range(2):
-                    nc.gpsimd.tensor_scalar(
+                    nc.vector.tensor_scalar(
                         out=o[:, v, h, :],
                         in0=st["ex", m][:, v, h, :],
                         scalar1=st["ri", m][:, v, h : h + 1],
-                        scalar2=0.0,
+                        scalar2=None,
                         op0=ALU.mult,
-                        op1=ALU.add,
                     )
             nc.sync.dma_start(
                 out=out[m, v0:v1].rearrange("v (p f) j -> p v (f j)", f=2),

@@ -24,7 +24,7 @@ AX = mybir.AxisListType
 
 FLOPS = 2 * B * S * D * N_OUT * 2 + 2 * B * H * S * S * D
 
-X_CHUNKS = (2, 2, 4, 8, 8, 8)
+X_CHUNKS = (1, 1, 2, 4, 8, 8, 8)
 
 
 def tile_bertselfattention_pa_t_w4_kernel(
@@ -80,66 +80,70 @@ def tile_bertselfattention_pa_t_w4_kernel(
                     out=raw_s[32 * q : 32 * q + 4, w * N_OUT : (w + 1) * N_OUT].bitcast(I32),
                     in_=scales[0, 4 * q : 4 * q + 4, :].bitcast(I32),
                 )
-        for i in range(1, len(X_CHUNKS)):
+            load_x(1 + w)
+        for i in range(3, len(X_CHUNKS)):
             load_x(i)
 
         w_codes = []
         w_scales = []
 
-        def permute(w):
-            wc = keep.tile([P, 2 * N_OUT], U8, name="wc%d" % w, align_bytes=64)
-            ws = keep.tile([P, N_OUT], U8, name="ws%d" % w, align_bytes=64)
-            dst_c = wc[:].bitcast(I32).rearrange("p (h t q c) -> p h q t c", h=2, t=4, q=16)
-            src_c = raw_w[w][:].bitcast(I32).rearrange("p (h q t c) -> p h q t c", h=2, t=4, q=16)
-            dst_s = ws[:].bitcast(I32).rearrange("p (h t q c) -> p h q t c", h=2, t=4, q=16)
-            src_s = (
-                raw_s[:, w * N_OUT : (w + 1) * N_OUT]
-                .bitcast(I32)
-                .rearrange("p (h q t c) -> p h q t c", h=2, t=4, q=16)
+        for w in range(2):
+            w_codes.append(keep.tile([P, 2 * N_OUT], U8, name="wc%d" % w, align_bytes=64))
+            w_scales.append(keep.tile([P, N_OUT], U8, name="ws%d" % w, align_bytes=64))
+
+        def permute(w, h):
+            order = "p (h q t c) -> p h q t c"
+            new_order = "p (h t q c) -> p h q t c"
+            nc.vector.tensor_copy(
+                out=w_codes[w][:].bitcast(I32).rearrange(new_order, h=2, t=4, q=16)[:, h],
+                in_=raw_w[w][:].bitcast(I32).rearrange(order, h=2, t=4, q=16)[:, h],
             )
-            for h in range(2):
-                nc.vector.tensor_copy(out=dst_c[:, h], in_=src_c[:, h])
-                nc.vector.tensor_copy(out=dst_s[:, h], in_=src_s[:, h])
-            w_codes.append(wc)
-            w_scales.append(ws)
+            nc.vector.tensor_copy(
+                out=w_scales[w][:].bitcast(I32).rearrange(new_order, h=2, t=4, q=16)[:, h],
+                in_=raw_s[:, w * N_OUT : (w + 1) * N_OUT]
+                .bitcast(I32)
+                .rearrange(order, h=2, t=4, q=16)[:, h],
+            )
 
         st = {}
 
-        def cast(u):
+        def cast(u, n, engine_copy):
             xbytes, j = x_of[u]
             xb = work.tile([P, 2 * D], BF16, name="xb", align_bytes=64)
-            nc.vector.tensor_copy(out=xb[:], in_=xbytes[:, j * D : (j + 2) * D].bitcast(FP8))
+            engine_copy(out=xb[:, : n * D], in_=xbytes[:, j * D : (j + n) * D].bitcast(FP8))
             st["xb", u] = xb
 
-        def trans(u):
-            tr = ps_tr.tile([P, 2, 2, P], F32, name="tr")
+        def trans(u, n):
+            tr = ps_tr.tile([P, 2, 2 * P], F32, name="tr")
             words = st["xb", u][:].bitcast(F32)
-            for v in range(2):
+            for v in range(n):
                 for e in range(2):
                     nc.tensor.transpose(
-                        tr[:, e, v, :], words[:, v * (D // 2) + e : (v + 1) * (D // 2) : 2], ident[:]
+                        tr[:, e, v * P : (v + 1) * P],
+                        words[:, v * (D // 2) + e : (v + 1) * (D // 2) : 2],
+                        ident[:],
                     )
             st["tr", u] = tr
 
-        def mult(u):
+        def mult(u, n):
             xg = work.tile([P, 2 * P, PACK], BF16, name="xg", align_bytes=64)
             nc.vector.tensor_tensor(
-                out=xg[:].rearrange("p n (e c) -> p n e c", e=2),
-                in0=st["tr", u][:].rearrange("p e v n -> p e (v n)").bitcast(BF16).rearrange("p e (n c) -> p n e c", c=2),
-                in1=xs_col[:].rearrange("p (e c) -> p e c", e=2).unsqueeze(1).to_broadcast([P, 2 * P, 2, 2]),
+                out=xg[:, : n * P].rearrange("p n (e c) -> p n e c", e=2),
+                in0=st["tr", u][:].bitcast(BF16)[:, :, : 2 * n * P].rearrange("p e (n c) -> p n e c", c=2),
+                in1=xs_col[:].rearrange("p (e c) -> p e c", e=2).unsqueeze(1).to_broadcast([P, n * P, 2, 2]),
                 op=ALU.mult,
             )
             st["xg", u] = xg
 
-        def quant_x(u):
+        def quant_x(u, n):
             xc = work.tile([P, 2 * P], U32, name="xc", align_bytes=64)
             xs = work.tile([P, 2 * P], U8, name="xs", align_bytes=64)
             nc.vector.quantize_mx(
-                out=xc[:].bitcast(FP8X4),
-                scales=xs[:],
-                in_=st["xg", u][:].rearrange("p n t -> p (n t)"),
+                out=xc[:, : n * P].bitcast(FP8X4),
+                scales=xs[:, : n * P],
+                in_=st["xg", u][:, : n * P].rearrange("p n t -> p (n t)"),
             )
-            for v in range(2):
+            for v in range(n):
                 st["xq", u + v] = (xc[:, v * P : (v + 1) * P], xs[:, v * P : (v + 1) * P])
 
         def proj(u, c):
@@ -160,11 +164,11 @@ def tile_bertselfattention_pa_t_w4_kernel(
             st["pj", u, c] = pj
 
         def copy(u, c):
-            if c == 0:
+            if ("qk", u) not in st:
                 st["qk", u] = work.tile([P, 4, P, PACK], BF16, name="qk", align_bytes=64)
             dst = st["qk", u][:, c]
             src = st["pj", u, c][:].rearrange("p t n -> p n t")
-            if False:
+            if (u, c) in on_vector:
                 nc.vector.tensor_copy(out=dst, in_=src)
             else:
                 nc.scalar.copy(out=dst, in_=src)
@@ -194,103 +198,182 @@ def tile_bertselfattention_pa_t_w4_kernel(
                 )
             st["sc", u] = sc
 
-        def rowmax(u):
-            mx = small.tile([P, 2], F32, name="mx")
-            nc.vector.tensor_reduce(out=mx[:], in_=st["sc", u][:], axis=AX.X, op=ALU.max)
-            st["mx", u] = mx
-
-        def negb(u):
-            nb = small.tile([P, 2], F32, name="nb")
-            nc.vector.tensor_scalar(
-                out=nb[:], in0=st["mx", u][:], scalar1=-inv, scalar2=None, op0=ALU.mult
+        def rowmax(u, h0, h1):
+            if h0 == 0:
+                st["mx", u] = small.tile([P, 2], F32, name="mx")
+                st["nb", u] = small.tile([P, 2], F32, name="nb")
+            nc.vector.tensor_reduce(
+                out=st["mx", u][:, h0:h1], in_=st["sc", u][:, h0:h1], axis=AX.X, op=ALU.max
             )
-            st["nb", u] = nb
+
+        def negb(u, h0, h1):
+            nc.vector.tensor_scalar(
+                out=st["nb", u][:, h0:h1], in0=st["mx", u][:, h0:h1], scalar1=-inv, scalar2=None, op0=ALU.mult
+            )
 
         def expo(u, h):
-            v = u % 2
+            m, v = divmod(u, 2)
             if h == 0 and v == 0:
-                st["ex", u // 2] = work.tile([P, 2, 2, S], F32, name="ex", align_bytes=64)
-                st["sm", u // 2] = small.tile([P, 2, 2], F32, name="sm")
+                st["ex", m] = work.tile([P, 4, S], F32, name="ex", align_bytes=64)
+                st["sm", m] = small.tile([P, 4], F32, name="sm")
+                st["ri", m] = small.tile([P, 4], F32, name="ri")
+                st["o", m] = work.tile([P, 4, S], F32, name="o", align_bytes=64)
             nc.scalar.activation(
-                out=st["ex", u // 2][:, v, h, :].rearrange("p (n g) -> p n g", g=2),
+                out=st["ex", m][:, 2 * v + h, :].rearrange("p (n g) -> p n g", g=2),
                 in_=st["sc", u][:, h, :].rearrange("p (g n) -> p n g", g=2),
                 func=ACT.Exp,
                 bias=st["nb", u][:, h : h + 1],
                 scale=inv,
-                accum_out=st["sm", u // 2][:, v, h : h + 1],
+                accum_out=st["sm", m][:, 2 * v + h : 2 * v + h + 1],
             )
 
-        def recip(m, v0, v1):
-            if v0 == 0:
-                st["ri", m] = small.tile([P, 2, 2], F32, name="ri")
-            nc.vector.reciprocal(out=st["ri", m][:, v0:v1, :], in_=st["sm", m][:, v0:v1, :])
+        def recip(m, r0, r1):
+            nc.vector.reciprocal(out=st["ri", m][:, r0:r1], in_=st["sm", m][:, r0:r1])
 
-        def norm(m, v0, v1):
-            if v0 == 0:
-                st["o", m] = work.tile([P, 2, 2, S], F32, name="o", align_bytes=64)
-            o = st["o", m]
-            for v in range(v0, v1):
-                for h in range(2):
-                    nc.vector.tensor_scalar(
-                        out=o[:, v, h, :],
-                        in0=st["ex", m][:, v, h, :],
-                        scalar1=st["ri", m][:, v, h : h + 1],
-                        scalar2=None,
-                        op0=ALU.mult,
-                    )
+        def norm_gpsimd(m, r):
+            nc.gpsimd.tensor_scalar(
+                out=st["o", m][:, r, :],
+                in0=st["ex", m][:, r, :],
+                scalar1=st["ri", m][:, r : r + 1],
+                scalar2=0.0,
+                op0=ALU.mult,
+                op1=ALU.add,
+            )
+
+        def norm(m, r0, r1):
+            for r in range(r0, r1):
+                nc.vector.tensor_scalar(
+                    out=st["o", m][:, r, :],
+                    in0=st["ex", m][:, r, :],
+                    scalar1=st["ri", m][:, r : r + 1],
+                    scalar2=None,
+                    op0=ALU.mult,
+                )
+
+        def store(m, v0, v1):
             nc.sync.dma_start(
                 out=out[m, v0:v1].rearrange("v (p f) j -> p v (f j)", f=2),
-                in_=o[:, v0:v1].rearrange("p v f j -> p v (f j)"),
+                in_=st["o", m][:, 2 * v0 : 2 * v1, :].rearrange("p (v f) j -> p v (f j)", f=2),
+            )
+
+        def store_half(m, v, f):
+            nc.sync.dma_start(
+                out=out[m, v].rearrange("(p f) j -> p f j", f=2)[:, f], in_=st["o", m][:, 2 * v + f, :]
             )
 
         def live(u):
             return 0 <= u < UNITS
 
-        for s in range(-3, UNITS + 3):
-            odd = s % 2 == 1
-            if live(s - 1):
+        on_vector = set()
+        for u in range(UNITS):
+            for c in range(4):
+                if u % 2 == 1 and c == 2 or u == UNITS - 1 and c == 3:
+                    on_vector.add((u, c))
+
+        cast(0, 1, nc.vector.tensor_copy)
+        cast(1, 1, nc.scalar.copy)
+        trans(0, 1)
+        mult(0, 1)
+        permute(0, 0)
+        quant_x(0, 1)
+        trans(1, 1)
+        permute(0, 1)
+        mult(1, 1)
+        proj(0, 0)
+        cast(2, 2, nc.scalar.copy)
+        permute(1, 0)
+        quant_x(1, 1)
+        permute(1, 1)
+        for c in range(1, 4):
+            proj(0, c)
+        trans(2, 2)
+
+        for s in range(UNITS):
+            first, more = live(s - 1), live(s + 1)
+            if first:
                 quant_qk(s - 1)
-            if live(s + 1):
-                proj(s + 1, 0)
-            if live(s - 1):
-                scores(s - 1)
-            if odd and live(s + 3):
-                cast(s + 3)
-            if not odd and live(s + 2):
-                mult(s + 2)
-            if live(s):
+            if s % 2 == 0:
+                m = s // 2
+                if more:
+                    proj(s + 1, 0)
+                if first:
+                    scores(s - 1)
                 copy(s, 0)
-            if live(s - 1):
-                rowmax(s - 1)
-                negb(s - 1)
-            if live(s - 2):
-                expo(s - 2, 0)
-            if live(s + 1):
-                proj(s + 1, 1)
-            if live(s):
+                if m >= 2:
+                    norm_gpsimd(m - 2, 0)
                 copy(s, 1)
-            if live(s - 2):
-                expo(s - 2, 1)
-            if live(s):
                 copy(s, 2)
-            if live(s + 1):
-                proj(s + 1, 2)
-            if odd and live(s + 3):
-                trans(s + 3)
-            if not odd and live(s + 2):
-                quant_x(s + 2)
-            if s == -3:
-                permute(0)
-            if s == -2:
-                permute(1)
-            if live(s):
+                if live(s + 2):
+                    mult(s + 2, 2)
+                if more:
+                    proj(s + 1, 1)
+                if first:
+                    rowmax(s - 1, 0, 2)
                 copy(s, 3)
-            if live(s + 1):
-                proj(s + 1, 3)
-            if live(s - 2):
-                if s - 2 >= UNITS - 2:
-                    recip((s - 2) // 2, s % 2, s % 2 + 1)
-                    norm((s - 2) // 2, s % 2, s % 2 + 1)
-                elif odd:
-                    recip((s - 2) // 2, 0, 2)
-                    norm((s - 2) // 2, 0, 2)
+                if more:
+                    proj(s + 1, 2)
+                if live(s - 2):
+                    expo(s - 2, 0)
+                if more:
+                    proj(s + 1, 3)
+                if live(s + 4):
+                    cast(s + 4, 2, nc.gpsimd.tensor_copy)
+                    trans(s + 4, 2)
+                if live(s - 2):
+                    expo(s - 2, 1)
+                if live(s + 2):
+                    quant_x(s + 2, 2)
+                if first:
+                    negb(s - 1, 0, 2)
+            else:
+                m = (s - 5) // 2
+                copy(s, 2)
+                if m >= 0:
+                    norm_gpsimd(m, 1)
+                copy(s, 0)
+                copy(s, 1)
+                if live(s - 2):
+                    expo(s - 2, 0)
+                if m >= 0:
+                    norm_gpsimd(m, 2)
+                if live(s - 2):
+                    expo(s - 2, 1)
+                if more:
+                    proj(s + 1, 0)
+                scores(s - 1)
+                if more:
+                    proj(s + 1, 1)
+                rowmax(s - 1, 0, 2)
+                if m >= 0:
+                    norm_gpsimd(m, 3)
+                    store(m, 0, 2)
+                copy(s, 3)
+                if more:
+                    proj(s + 1, 2)
+                    proj(s + 1, 3)
+                negb(s - 1, 0, 2)
+                if live(s - 3):
+                    recip((s - 3) // 2, 0, 4)
+
+        last = UNITS - 1
+        m = last // 2
+        quant_qk(last)
+        scores(last)
+        expo(last - 1, 0)
+        norm(m - 1, 0, 4)
+        store(m - 1, 0, 2)
+        expo(last - 1, 1)
+        rowmax(last, 0, 1)
+        recip(m, 0, 2)
+        negb(last, 0, 1)
+        rowmax(last, 1, 2)
+        norm(m, 0, 1)
+        negb(last, 1, 2)
+        expo(last, 0)
+        expo(last, 1)
+        norm(m, 1, 2)
+        store(m, 0, 1)
+        for f in range(2):
+            recip(m, 2 + f, 3 + f)
+            norm(m, 2 + f, 3 + f)
+            store_half(m, 1, f)

import math
from contextlib import ExitStack

import concourse.mybir as mybir
from concourse.masks import make_identity

B, S, D, H = 16, 256, 512, 2
P = 128
PACK = 4
UNITS = B * H
N_OUT = H * D

F32 = mybir.dt.float32
BF16 = mybir.dt.bfloat16
I32 = mybir.dt.int32
U32 = mybir.dt.uint32
U8 = mybir.dt.uint8
FP8 = mybir.dt.float8_e4m3fn
FP8X4 = mybir.dt.float8_e4m3fn_x4
FP4X4 = mybir.dt.float4_e2m1fn_x4
ACT = mybir.ActivationFunctionType
ALU = mybir.AluOpType
AX = mybir.AxisListType

FLOPS = 2 * B * S * D * N_OUT * 2 + 2 * B * H * S * S * D

X_CHUNKS = (1, 1, 2, 4, 8, 8, 8)


def tile_bertselfattention_pa_t_w4_kernel(
    tc, x_bytes, x_scale, wq_words, wq_scales, wk_words, wk_scales, out
):
    nc = tc.nc
    inv = 1.0 / math.sqrt(D)

    with ExitStack() as ctx:
        keep = ctx.enter_context(tc.tile_pool(name="keep", bufs=1))
        xin = ctx.enter_context(tc.tile_pool(name="xin", bufs=1))
        work = ctx.enter_context(tc.tile_pool(name="work", bufs=3))
        small = ctx.enter_context(tc.tile_pool(name="small", bufs=4))
        ps_tr = ctx.enter_context(tc.psum_pool(name="ps_tr", bufs=1))
        ps_pj = ctx.enter_context(tc.psum_pool(name="ps_pj", bufs=5))
        ps_sc = ctx.enter_context(tc.psum_pool(name="ps_sc", bufs=2))
        ctx.enter_context(tc.manual_schedule())

        x_view = x_bytes.rearrange("b (h p) k -> p (b h) k", p=P)
        x_of = {}

        def load_x(i):
            u0 = sum(X_CHUNKS[:i])
            n = X_CHUNKS[i]
            xbytes = xin.tile([P, n * D], U8, name="xbytes%d" % i, align_bytes=64)
            nc.sync.dma_start(
                out=xbytes[:].rearrange("p (u k) -> p u k", u=n), in_=x_view[:, u0 : u0 + n, :]
            )
            for j in range(n):
                x_of[u0 + j] = (xbytes, j)

        raw_s = keep.tile([P, 2 * N_OUT], U8, name="raw_s", align_bytes=64)
        nc.vector.memset(raw_s[:].bitcast(I32), 0)
        xs_col = keep.tile([P, PACK], F32, name="xs_col")
        nc.scalar.dma_start(
            out=xs_col[:], in_=x_scale.rearrange("a o (p t) -> p (a o t)", t=PACK)
        )
        ident = keep.tile([P, P], F32, name="ident", align_bytes=64)
        make_identity(nc, ident[:])
        warm = keep.tile([P, 1], F32, name="warm")
        nc.vector.memset(warm[:], 0.0)
        warm_out = keep.tile([P, 1], F32, name="warm_out")
        nc.scalar.activation(out=warm_out[:], in_=warm[:], func=ACT.Exp)

        load_x(0)
        raw_w = []
        for w, (words, scales) in enumerate(((wq_words, wq_scales), (wk_words, wk_scales))):
            rw = keep.tile([P, 2 * N_OUT], U8, name="raw_w%d" % w, align_bytes=64)
            nc.sync.dma_start(out=rw[:].bitcast(I32), in_=words[0].bitcast(I32))
            raw_w.append(rw)
            for q in range(4):
                nc.sync.dma_start(
                    out=raw_s[32 * q : 32 * q + 4, w * N_OUT : (w + 1) * N_OUT].bitcast(I32),
                    in_=scales[0, 4 * q : 4 * q + 4, :].bitcast(I32),
                )
            load_x(1 + w)
        for i in range(3, len(X_CHUNKS)):
            load_x(i)

        w_codes = []
        w_scales = []

        for w in range(2):
            w_codes.append(keep.tile([P, 2 * N_OUT], U8, name="wc%d" % w, align_bytes=64))
            w_scales.append(keep.tile([P, N_OUT], U8, name="ws%d" % w, align_bytes=64))

        def permute(w, h):
            order = "p (h q t c) -> p h q t c"
            new_order = "p (h t q c) -> p h q t c"
            nc.vector.tensor_copy(
                out=w_codes[w][:].bitcast(I32).rearrange(new_order, h=2, t=4, q=16)[:, h],
                in_=raw_w[w][:].bitcast(I32).rearrange(order, h=2, t=4, q=16)[:, h],
            )
            nc.vector.tensor_copy(
                out=w_scales[w][:].bitcast(I32).rearrange(new_order, h=2, t=4, q=16)[:, h],
                in_=raw_s[:, w * N_OUT : (w + 1) * N_OUT]
                .bitcast(I32)
                .rearrange(order, h=2, t=4, q=16)[:, h],
            )

        st = {}

        def cast(u, n, engine_copy):
            xbytes, j = x_of[u]
            xb = work.tile([P, 2 * D], BF16, name="xb", align_bytes=64)
            engine_copy(out=xb[:, : n * D], in_=xbytes[:, j * D : (j + n) * D].bitcast(FP8))
            st["xb", u] = xb

        def trans(u, n):
            tr = ps_tr.tile([P, 2, 2 * P], F32, name="tr")
            words = st["xb", u][:].bitcast(F32)
            for v in range(n):
                for e in range(2):
                    nc.tensor.transpose(
                        tr[:, e, v * P : (v + 1) * P],
                        words[:, v * (D // 2) + e : (v + 1) * (D // 2) : 2],
                        ident[:],
                    )
            st["tr", u] = tr

        def mult(u, n):
            xg = work.tile([P, 2 * P, PACK], BF16, name="xg", align_bytes=64)
            nc.vector.tensor_tensor(
                out=xg[:, : n * P].rearrange("p n (e c) -> p n e c", e=2),
                in0=st["tr", u][:].bitcast(BF16)[:, :, : 2 * n * P].rearrange("p e (n c) -> p n e c", c=2),
                in1=xs_col[:].rearrange("p (e c) -> p e c", e=2).unsqueeze(1).to_broadcast([P, n * P, 2, 2]),
                op=ALU.mult,
            )
            st["xg", u] = xg

        def quant_x(u, n):
            xc = work.tile([P, 2 * P], U32, name="xc", align_bytes=64)
            xs = work.tile([P, 2 * P], U8, name="xs", align_bytes=64)
            nc.vector.quantize_mx(
                out=xc[:, : n * P].bitcast(FP8X4),
                scales=xs[:, : n * P],
                in_=st["xg", u][:, : n * P].rearrange("p n t -> p (n t)"),
            )
            for v in range(n):
                st["xq", u + v] = (xc[:, v * P : (v + 1) * P], xs[:, v * P : (v + 1) * P])

        def proj(u, c):
            w, h = divmod(c, 2)
            xc, xs = st["xq", u]
            pj = ps_pj.tile([P, PACK, P], F32, name="pj")
            for t in range(PACK):
                col = (h * PACK + t) * P
                nc.tensor.matmul_mx(
                    out=pj[:, t, :],
                    lhsT=w_codes[w][:, 2 * col : 2 * (col + P)].bitcast(FP4X4),
                    lhsT_scale=w_scales[w][:, col : col + P],
                    rhs=xc.bitcast(FP8X4),
                    rhs_scale=xs,
                    start=True,
                    stop=True,
                )
            st["pj", u, c] = pj

        def copy(u, c):
            if ("qk", u) not in st:
                st["qk", u] = work.tile([P, 4, P, PACK], BF16, name="qk", align_bytes=64)
            dst = st["qk", u][:, c]
            src = st["pj", u, c][:].rearrange("p t n -> p n t")
            if (u, c) in on_vector:
                nc.vector.tensor_copy(out=dst, in_=src)
            else:
                nc.scalar.copy(out=dst, in_=src)

        def quant_qk(u):
            qc = work.tile([P, 4 * P], U32, name="qc", align_bytes=64)
            qs = work.tile([P, 4 * P], U8, name="qs", align_bytes=64)
            nc.vector.quantize_mx(
                out=qc[:].bitcast(FP8X4),
                scales=qs[:],
                in_=st["qk", u][:].rearrange("p c n t -> p (c n t)"),
            )
            st["qq", u] = (qc, qs)

        def scores(u):
            qc, qs = st["qq", u]
            sc = ps_sc.tile([P, 2, S], F32, name="sc")
            for h in range(2):
                nc.tensor.matmul_mx(
                    out=sc[:, h, :],
                    lhsT=qc[:, h * P : (h + 1) * P].bitcast(FP8X4),
                    lhsT_scale=qs[:, h * P : (h + 1) * P],
                    rhs=qc[:, 2 * P : 4 * P].bitcast(FP8X4),
                    rhs_scale=qs[:, 2 * P : 4 * P],
                    start=True,
                    stop=True,
                )
            st["sc", u] = sc

        def rowmax(u, h0, h1):
            if h0 == 0:
                st["mx", u] = small.tile([P, 2], F32, name="mx")
                st["nb", u] = small.tile([P, 2], F32, name="nb")
            nc.vector.tensor_reduce(
                out=st["mx", u][:, h0:h1], in_=st["sc", u][:, h0:h1], axis=AX.X, op=ALU.max
            )

        def negb(u, h0, h1):
            nc.vector.tensor_scalar(
                out=st["nb", u][:, h0:h1], in0=st["mx", u][:, h0:h1], scalar1=-inv, scalar2=None, op0=ALU.mult
            )

        def expo(u, h):
            m, v = divmod(u, 2)
            if h == 0 and v == 0:
                st["ex", m] = work.tile([P, 4, S], F32, name="ex", align_bytes=64)
                st["sm", m] = small.tile([P, 4], F32, name="sm")
                st["ri", m] = small.tile([P, 4], F32, name="ri")
                st["o", m] = work.tile([P, 4, S], F32, name="o", align_bytes=64)
            nc.scalar.activation(
                out=st["ex", m][:, 2 * v + h, :].rearrange("p (n g) -> p n g", g=2),
                in_=st["sc", u][:, h, :].rearrange("p (g n) -> p n g", g=2),
                func=ACT.Exp,
                bias=st["nb", u][:, h : h + 1],
                scale=inv,
                accum_out=st["sm", m][:, 2 * v + h : 2 * v + h + 1],
            )

        def recip(m, r0, r1):
            nc.vector.reciprocal(out=st["ri", m][:, r0:r1], in_=st["sm", m][:, r0:r1])

        def norm_gpsimd(m, r):
            nc.gpsimd.tensor_scalar(
                out=st["o", m][:, r, :],
                in0=st["ex", m][:, r, :],
                scalar1=st["ri", m][:, r : r + 1],
                scalar2=0.0,
                op0=ALU.mult,
                op1=ALU.add,
            )

        def norm(m, r0, r1):
            for r in range(r0, r1):
                nc.vector.tensor_scalar(
                    out=st["o", m][:, r, :],
                    in0=st["ex", m][:, r, :],
                    scalar1=st["ri", m][:, r : r + 1],
                    scalar2=None,
                    op0=ALU.mult,
                )

        def store(m, v0, v1):
            nc.sync.dma_start(
                out=out[m, v0:v1].rearrange("v (p f) j -> p v (f j)", f=2),
                in_=st["o", m][:, 2 * v0 : 2 * v1, :].rearrange("p (v f) j -> p v (f j)", f=2),
            )

        def store_half(m, v, f):
            nc.sync.dma_start(
                out=out[m, v].rearrange("(p f) j -> p f j", f=2)[:, f], in_=st["o", m][:, 2 * v + f, :]
            )

        def live(u):
            return 0 <= u < UNITS

        on_vector = set()
        for u in range(UNITS):
            for c in range(4):
                if u % 2 == 1 and c == 2 or u == UNITS - 1 and c == 3:
                    on_vector.add((u, c))

        cast(0, 1, nc.vector.tensor_copy)
        cast(1, 1, nc.scalar.copy)
        trans(0, 1)
        mult(0, 1)
        permute(0, 0)
        quant_x(0, 1)
        trans(1, 1)
        permute(0, 1)
        mult(1, 1)
        proj(0, 0)
        cast(2, 2, nc.scalar.copy)
        permute(1, 0)
        quant_x(1, 1)
        permute(1, 1)
        for c in range(1, 4):
            proj(0, c)
        trans(2, 2)

        for s in range(UNITS):
            first, more = live(s - 1), live(s + 1)
            if first:
                quant_qk(s - 1)
            if s % 2 == 0:
                m = s // 2
                if more:
                    proj(s + 1, 0)
                if first:
                    scores(s - 1)
                copy(s, 0)
                if m >= 2:
                    norm_gpsimd(m - 2, 0)
                copy(s, 1)
                copy(s, 2)
                if live(s + 2):
                    mult(s + 2, 2)
                if more:
                    proj(s + 1, 1)
                if first:
                    rowmax(s - 1, 0, 2)
                copy(s, 3)
                if more:
                    proj(s + 1, 2)
                if live(s - 2):
                    expo(s - 2, 0)
                if more:
                    proj(s + 1, 3)
                if live(s + 4):
                    cast(s + 4, 2, nc.gpsimd.tensor_copy)
                    trans(s + 4, 2)
                if live(s - 2):
                    expo(s - 2, 1)
                if live(s + 2):
                    quant_x(s + 2, 2)
                if first:
                    negb(s - 1, 0, 2)
            else:
                m = (s - 5) // 2
                copy(s, 2)
                if m >= 0:
                    norm_gpsimd(m, 1)
                copy(s, 0)
                copy(s, 1)
                if live(s - 2):
                    expo(s - 2, 0)
                if m >= 0:
                    norm_gpsimd(m, 2)
                if live(s - 2):
                    expo(s - 2, 1)
                if more:
                    proj(s + 1, 0)
                scores(s - 1)
                if more:
                    proj(s + 1, 1)
                rowmax(s - 1, 0, 2)
                if m >= 0:
                    norm_gpsimd(m, 3)
                    store(m, 0, 2)
                copy(s, 3)
                if more:
                    proj(s + 1, 2)
                    proj(s + 1, 3)
                negb(s - 1, 0, 2)
                if live(s - 3):
                    recip((s - 3) // 2, 0, 4)

        last = UNITS - 1
        m = last // 2
        quant_qk(last)
        scores(last)
        expo(last - 1, 0)
        norm(m - 1, 0, 4)
        store(m - 1, 0, 2)
        expo(last - 1, 1)
        rowmax(last, 0, 1)
        recip(m, 0, 2)
        negb(last, 0, 1)
        rowmax(last, 1, 2)
        norm(m, 0, 1)
        negb(last, 1, 2)
        expo(last, 0)
        expo(last, 1)
        norm(m, 1, 2)
        store(m, 0, 1)
        for f in range(2):
            recip(m, 2 + f, 3 + f)
            norm(m, 2 + f, 3 + f)
            store_half(m, 1, f)
